import numpy as np
import ml_dtypes


def mxq(x, axis, fmt="e4m3"):
    dtype, down = {"e4m3": (ml_dtypes.float8_e4m3fn, 7), "e5m2": (ml_dtypes.float8_e5m2, 14)}[fmt]
    v = np.moveaxis(np.asarray(x, np.float32).astype(ml_dtypes.bfloat16).astype(np.float64), axis, -1)
    blocks = v.reshape(v.shape[:-1] + (-1, 32))
    amax = np.abs(blocks).max(-1, keepdims=True)
    byte = np.maximum(np.where(amax > 0, np.frexp(amax)[1] - 1 + 127, 0) - down, 1)
    scale = np.exp2(byte - 127.0)
    codes = (blocks / scale).astype(np.float32).astype(dtype).astype(np.float64)
    return np.moveaxis((codes * scale).reshape(v.shape), -1, axis)


WIDE = False


def mx_kscale(k):
    if not WIDE:
        return np.ones(k)
    levels = np.array([10, -10, 5, -5, 0])
    if k % 512:
        return np.exp2(np.random.permutation(np.resize(levels, k // 32))).repeat(32)
    a = np.empty((k // 512, 16))
    for p in range(k // 512):
        a[p, :8] = np.random.permutation(np.resize(levels, 8))
        for g in range(8):
            far = levels[np.abs(levels - a[p, g]) >= 10]
            a[p, g + 8] = far[np.random.randint(len(far))]
    return np.exp2(a.ravel()).repeat(32)


BF16 = ml_dtypes.bfloat16


def bf(x):
    return np.asarray(x, np.float32).astype(BF16)


def f64(x):
    return np.asarray(x).astype(np.float64)


B, T, C, H = 2, 512, 1024, 8
DH = C // H


def rope_tables():
    i = f64(np.arange(1, DH // 2 + 1))
    thetas = np.repeat(1000.0 ** (-2.0 * i / DH), 2)
    pos = f64(np.arange(1, T + 1))
    args = pos[:, None] * thetas[None, :]
    return np.sin(args), np.cos(args)


def apply_rope(u, sin, cos):
    u_odd = u[..., ::2]
    u_even = u[..., 1::2]
    u_sin = np.stack([-u_even, u_odd], axis=-1).reshape(u.shape)
    return u * cos + u_sin * sin


def draw0():
    s = mx_kscale(C)
    return {"x": bf(np.random.standard_normal((B, T, C)) * s),
            "w_qk": bf(np.random.standard_normal((2 * C, C)) / np.sqrt(C) / s[None, :])}


def core(x, w_qk):
    qk = mxq(f64(x), 2, "e4m3") @ mxq(f64(w_qk), 1, "e4m3").T
    q, k = np.split(qk, 2, axis=-1)
    q = q.reshape(B, T, H, DH).transpose(0, 2, 1, 3)
    k = k.reshape(B, T, H, DH).transpose(0, 2, 1, 3)
    sin, cos = rope_tables()
    return q, k, apply_rope(q, sin, cos), apply_rope(k, sin, cos)


def e4m3fn_bytes(y):
    return np.clip(np.asarray(y, np.float64), -448.0, 448.0).astype(np.float32).astype(ml_dtypes.float8_e4m3fn).view(np.uint8)


def e4m3fn_values(b):
    return np.asarray(b, np.uint8).view(ml_dtypes.float8_e4m3fn).astype(np.float64)


def setup_inputs():
    d = draw0()
    x0 = np.asarray(d['w_qk']).astype(np.float64)
    s = (np.max(np.abs(x0), axis=(0,), keepdims=True) / 448.0).astype(np.float32)
    out = {}
    for k, v in d.items():
        if k == 'w_qk':
            out['w_qk_bytes'] = e4m3fn_bytes(x0 / s.astype(np.float64))
            out['w_qk_scale'] = s
        else:
            out[k] = v
    return out


def reference(x, w_qk_bytes, w_qk_scale):
    return core(x, e4m3fn_values(w_qk_bytes) * w_qk_scale.astype(np.float64))

@@ -1,0 +1,319 @@
+from contextlib import ExitStack
+import math
+
+import concourse.mybir as mybir
+from concourse.masks import make_identity
+
+B, T, C, H, DH = 2, 512, 1024, 8, 128
+FLOPS = 2 * B * T * C * 2 * C
+
+F32 = mybir.dt.float32
+BF16 = mybir.dt.bfloat16
+U32 = mybir.dt.uint32
+U8 = mybir.dt.uint8
+I32 = mybir.dt.int32
+FP8 = mybir.dt.float8_e4m3fn
+FP8X4 = mybir.dt.float8_e4m3fn_x4
+ALU = mybir.AluOpType
+ACTF = mybir.ActivationFunctionType
+
+P = 128
+NCH = 512
+HALF = DH // 2
+
+
+def tile_ropeattnlayer_pa_kernel(tc, x, w_qk_bytes, w_qk_scale, out_0, out_1, out_2, out_3):
+    nc = tc.nc
+    with ExitStack() as ctx:
+        keep = ctx.enter_context(tc.tile_pool(name="keep", bufs=1))
+        wsp = ctx.enter_context(tc.tile_pool(name="wsp", bufs=8))
+        wcp = ctx.enter_context(tc.tile_pool(name="wcp", bufs=4))
+        gpl = ctx.enter_context(tc.tile_pool(name="gpl", bufs=3))
+        stg = ctx.enter_context(tc.tile_pool(name="stg", bufs=3))
+        tmp = ctx.enter_context(tc.tile_pool(name="tmp", bufs=4))
+        tpp = ctx.enter_context(tc.psum_pool(name="tpp", bufs=4))
+        mmp = ctx.enter_context(tc.psum_pool(name="mmp", bufs=4))
+        ctx.enter_context(tc.manual_schedule())
+
+        sc_bc = keep.tile([P, C], F32, name="sc_bc")
+        nc.sync.dma_start(out=sc_bc[:], in_=w_qk_scale.rearrange("o k -> (o k)").partition_broadcast(P))
+        sc4 = keep.tile([P, 2, 4], F32, name="sc4")
+        wb = []
+        for c in range(4):
+            wbt = keep.tile([P, 4, C], U8, name="wb%d" % c)
+            wb.append(wbt)
+        xs = []
+        for b in range(B):
+            for hf in range(2):
+                xst = keep.tile([P, 2, C], BF16, name="xs%d%d" % (b, hf))
+                xs.append(xst)
+
+        wb00 = keep.tile([P, C], U8, name="wb00")
+
+        def load_w(c, r0=0, r1=4):
+            wv = w_qk_bytes[NCH * c:NCH * (c + 1), :].rearrange("(r p) k -> p r k", p=P)
+            nc.sync.dma_start(out=wb[c][:, r0:r1, :], in_=wv[:, r0:r1, :])
+
+        def load_x(b):
+            xv = x[b].rearrange("(p i) k -> p i k", i=4)
+            for hf in range(2):
+                nc.sync.dma_start(out=xs[2 * b + hf][:], in_=xv[:, 2 * hf:2 * hf + 2, :])
+
+        nc.sync.dma_start(out=wb00[:], in_=w_qk_bytes[0:P, :])
+        load_w(0, 1, 4)
+        load_x(0)
+        load_w(1)
+        load_x(1)
+        nc.sync.dma_start(out=sc4[:], in_=w_qk_scale.rearrange("o (g p t) -> p (o g) t", p=P, t=4))
+        load_w(3)
+        load_w(2)
+
+        warm = keep.tile([P, 1], F32, name="warm")
+        warm2 = keep.tile([P, 1], F32, name="warm2")
+        nc.vector.memset(warm[:], 0.0)
+        nc.scalar.activation(out=warm2[:], in_=warm[:], func=ACTF.Sin)
+
+        q1 = 1000.0 ** (-2.0 / DH)
+        pos = keep.tile([P, 4, 1], F32, name="pos")
+        nc.gpsimd.iota(pos[:], pattern=[[1, 4]], base=1, channel_multiplier=4, allow_small_or_imprecise_dtypes=True)
+        ident = keep.tile([P, P], F32, name="ident")
+        make_identity(nc, ident[:])
+
+        tau = keep.tile([P, 4, HALF], F32, name="tau")
+        for j in range(4):
+            nc.vector.tensor_scalar(out=tau[:, :, j:j + 1], in0=pos[:], scalar1=q1 ** (j + 1) / (2.0 * math.pi),
+                                    scalar2=None, op0=ALU.mult)
+        w = 4
+        while w < HALF:
+            nc.vector.tensor_scalar(out=tau[:, :, w:2 * w], in0=tau[:, :, 0:w], scalar1=q1 ** w, scalar2=None,
+                                    op0=ALU.mult)
+            w *= 2
+        tau_f = tau[:].rearrange("p i j -> p (i j)")
+        kint = keep.tile([P, 4 * HALF], I32, name="kint")
+        kflt = keep.tile([P, 4 * HALF], F32, name="kflt")
+        frac = keep.tile([P, 2, 4 * HALF], F32, name="frac")
+        gneg = keep.tile([P, 2, 4, HALF], F32, name="gneg")
+        nc.vector.tensor_copy(out=kint[:], in_=tau_f)
+        nc.vector.tensor_copy(out=kflt[:], in_=kint[:])
+        nc.vector.tensor_tensor(out=frac[:, 0, :], in0=tau_f, in1=kflt[:], op=ALU.subtract)
+        nc.vector.tensor_scalar(out=frac[:, 1, :], in0=frac[:, 0, :], scalar1=0.25, scalar2=None, op0=ALU.add)
+
+        def fold():
+            ff = frac[:].rearrange("p s n -> p (s n)")
+            nc.vector.scalar_tensor_tensor(out=gneg[:].rearrange("p s i j -> p (s i j)"), in0=ff, scalar=0.5,
+                                           in1=ff, op0=ALU.is_gt, op1=ALU.subtract)
+
+        cosT = keep.tile([P, 4, HALF, 2], F32, name="cosT")
+        sinT = keep.tile([P, 4, HALF, 2], F32, name="sinT")
+
+        def sines():
+            nc.scalar.activation(out=cosT[:], in_=gneg[:, 1].unsqueeze(3).to_broadcast([P, 4, HALF, 2]),
+                                 func=ACTF.Sin, scale=-2.0 * math.pi)
+            nc.scalar.activation(out=sinT[:, :, :, 1:2], in_=gneg[:, 0].unsqueeze(3), func=ACTF.Sin,
+                                 scale=-2.0 * math.pi)
+            nc.scalar.activation(out=sinT[:, :, :, 0:1], in_=gneg[:, 0].unsqueeze(3), func=ACTF.Sin,
+                                 scale=2.0 * math.pi)
+
+        xcod, xscl, wcod, wscl = [], [], [], []
+        for b in range(B):
+            tcod = keep.tile([P, 2, NCH], U32, name="xcod%d" % b, align_bytes=64)
+            tscl = keep.tile([P, 2, NCH], U8, name="xscl%d" % b, align_bytes=64)
+            xcod.append(tcod)
+            xscl.append(tscl)
+        for c in range(4):
+            tcod = keep.tile([P, 2, NCH], U32, name="wcod%d" % c, align_bytes=64)
+            tscl = keep.tile([P, 2, NCH], U8, name="wscl%d" % c, align_bytes=64)
+            wcod.append(tcod)
+            wscl.append(tscl)
+
+        def wtt(c, r):
+            ws = wsp.tile([P, C], BF16, name="ws")
+            src = wb00[:] if (c == 0 and r == 0) else wb[c][:, r, :]
+            nc.vector.tensor_tensor(out=ws[:], in0=src.bitcast(FP8), in1=sc_bc[:], op=ALU.mult)
+            return ws[:]
+
+        def cast(c, r):
+            wc = wcp.tile([P, C], BF16, name="wc")
+            nc.scalar.copy(out=wc[:], in_=wb[c][:, r, :].bitcast(FP8))
+            return wc[:]
+
+        def new_grp():
+            grp = gpl.tile([P, 2, NCH, 4], BF16, name="grp", align_bytes=64)
+            return grp
+
+        def tr_pe(srcs, g, hf):
+            bank = tpp.tile([P, 2, 2, P], F32, name="bank")
+            for a in range(2):
+                words = srcs[2 * hf + a].bitcast(F32)
+                for u in range(2):
+                    nc.tensor.transpose(bank[:, a, u, :], words[:, 256 * g + u:256 * (g + 1):2], ident[:])
+            return bank
+
+        def tr_cp(bank, grp, g, hf):
+            gw = grp[:, g].rearrange("p c t -> p (c t)").bitcast(F32)
+            nc.scalar.copy(out=gw[:, 512 * hf:512 * (hf + 1)].rearrange("p (a q u) -> p a q u", a=2, u=2),
+                           in_=bank[:].rearrange("p a u q -> p a q u"))
+
+        def tr(srcs, grp, g, hf):
+            tr_cp(tr_pe(srcs, g, hf), grp, g, hf)
+
+        def trs_pe(srcs, g, u):
+            bank = tpp.tile([P, 4, P], F32, name="bank")
+            for r in range(4):
+                nc.tensor.transpose(bank[:, r, :], srcs[r].bitcast(F32)[:, 256 * g + u:256 * (g + 1):2], ident[:])
+            return bank
+
+        def trs_sc(bank, z, g, u, e):
+            src = bank[:].rearrange("p r q -> p (r q)").bitcast(BF16).rearrange("p (c e) -> p c e", e=2)
+            nc.scalar.activation(out=z[:, g, u, :, e], in_=src[:, :, e], func=ACTF.Copy,
+                                 scale=sc4[:, g, 2 * u + e:2 * u + e + 1])
+
+        def il(z, grp):
+            zin = z[:].rearrange("p g u c e -> p (g u c e)").bitcast(F32).rearrange("p (g u c) -> p g c u", g=2, u=2)
+            gout = grp[:].rearrange("p g c t -> p (g c t)").bitcast(F32).rearrange("p (g c u) -> p g c u", g=2, u=2)
+            nc.vector.tensor_copy(out=gout, in_=zin)
+
+        def qz(grp, cod, scl):
+            nc.vector.quantize_mx(out=cod[:].rearrange("p g c -> p (g c)").bitcast(FP8X4),
+                                  scales=scl[:].rearrange("p g c -> p (g c)"),
+                                  in_=grp[:].rearrange("p g c t -> p (g c t)"))
+
+        def x_srcs(b):
+            return [xs[2 * b + i // 2][:, i % 2, :] for i in range(4)]
+
+        def plain_unit(srcs):
+            grp = new_grp()
+            banks = []
+
+            def pe_run():
+                for hf in range(2):
+                    for g in range(2):
+                        banks.append(tr_pe(srcs, g, hf))
+
+            jobs = [[lambda k=k: tr_cp(banks[k], grp, k % 2, k // 2)] for k in range(4)]
+            return grp, pe_run, jobs
+
+        def group(b, c, pe_run=None, sjobs=None, vjobs=None, vd=(), splits=((0, 4),), rsplits=((0, 4),), a_first=()):
+            d_raw = out_0 if c < 2 else out_1
+            d_rope = out_2 if c < 2 else out_3
+            h0 = 4 * (c % 2)
+
+            def pieces(tag, cuts):
+                where = {}
+                for (i0, i1) in cuts:
+                    pt = stg.tile([P, 4, i1 - i0, DH], F32, name=(tag if i1 - i0 == 4 else tag + "h"))
+                    for i in range(i0, i1):
+                        where[i] = (pt, i0, i1)
+                return where
+
+            raws = pieces("raw", rsplits)
+            ropes = pieces("rope", splits)
+
+            def put(dst, where, i):
+                pt, i0, i1 = where[i]
+                if i == i1 - 1:
+                    nc.sync.dma_start(out=dst[b, h0:h0 + 4].rearrange("h (p i) d -> p h i d", i=4)[:, :, i0:i1, :],
+                                      in_=pt[:])
+
+            def copy_raw(i):
+                pt, i0, i1 = raws[i]
+                nc.scalar.copy(out=pt[:, :, i - i0, :], in_=accs[i][:].rearrange("p (h d) -> p h d", h=4))
+                put(d_raw, raws, i)
+
+            def add(eng, i, t1, t2):
+                pt, i0, i1 = ropes[i]
+                eng.tensor_tensor(out=pt[:, :, i - i0, :], in0=t1[:].rearrange("p h j e -> p h (j e)"),
+                                  in1=t2[:].rearrange("p h j e -> p h (j e)"), op=ALU.add)
+                put(d_rope, ropes, i)
+
+            accs = []
+            for i in range(4):
+                acc = mmp.tile([P, NCH], F32, name="acc")
+                accs.append(acc)
+                for g in range(2):
+                    nc.tensor.matmul_mx(out=acc[:], lhsT=xcod[b][:, g, i * P:(i + 1) * P].bitcast(FP8X4),
+                                        lhsT_scale=xscl[b][:, g, i * P:(i + 1) * P],
+                                        rhs=wcod[c][:, g, :].bitcast(FP8X4),
+                                        rhs_scale=wscl[c][:, g, :], start=(g == 0), stop=(g == 1))
+            if pe_run is not None:
+                pe_run()
+            late = []
+            for i in range(4):
+                t1 = tmp.tile([P, 4, HALF, 2], F32, name="t1")
+                t2 = tmp.tile([P, 4, HALF, 2], F32, name="t2")
+                a4 = accs[i][:].rearrange("p (h j e) -> p h j e", h=4, e=2)
+                if len(a_first) > 0 and i == a_first[0]:
+                    for k in a_first:
+                        copy_raw(k)
+                nc.vector.tensor_tensor(out=t1[:], in0=a4, in1=cosT[:, i].unsqueeze(1).to_broadcast([P, 4, HALF, 2]),
+                                        op=ALU.mult)
+                nc.vector.tensor_tensor(out=t2[:], in0=a4[:, :, :, ::-1],
+                                        in1=sinT[:, i].unsqueeze(1).to_broadcast([P, 4, HALF, 2]), op=ALU.mult)
+                if i not in a_first:
+                    copy_raw(i)
+                if vjobs is not None and i in vjobs:
+                    vjobs[i]()
+                if i in vd:
+                    late.append((i, t1, t2))
+                else:
+                    add(nc.gpsimd, i, t1, t2)
+                if sjobs is not None:
+                    for job in sjobs[i]:
+                        job()
+            for (i, t1, t2) in late:
+                add(nc.vector, i, t1, t2)
+
+        gx0 = new_grp()
+        gw0 = new_grp()
+        gw1 = new_grp()
+        s0 = [wtt(0, 0), wtt(0, 1)]
+        fold()
+        for hf in range(2):
+            for g in range(2):
+                tr(x_srcs(0), gx0, g, hf)
+        tr(s0, gw0, 0, 0)
+        tr(s0, gw0, 1, 0)
+        sines()
+        s0.append(wtt(0, 2))
+        s0.append(wtt(0, 3))
+        tr(s0, gw0, 0, 1)
+        tr(s0, gw0, 1, 1)
+        s1 = [wtt(1, 0), wtt(1, 1)]
+        tr(s1, gw1, 0, 0)
+        tr(s1, gw1, 1, 0)
+        s1.append(wtt(1, 2))
+        s1.append(wtt(1, 3))
+        tr(s1, gw1, 0, 1)
+        tr(s1, gw1, 1, 1)
+        qz(gx0, xcod[0], xscl[0])
+        qz(gw0, wcod[0], wscl[0])
+        qz(gw1, wcod[1], wscl[1])
+
+        gx1, run_x1, jobs_x1 = plain_unit(x_srcs(1))
+        group(0, 0, pe_run=run_x1, sjobs=jobs_x1)
+        c3 = []
+        group(0, 1, vjobs={0: lambda: qz(gx1, xcod[1], xscl[1])},
+              sjobs=[[lambda r=r: c3.append(cast(3, r))] for r in range(4)])
+        s2 = [wtt(2, r) for r in range(4)]
+        gw2, run_w2, jobs_w2 = plain_unit(s2)
+        group(1, 0, pe_run=run_w2, sjobs=jobs_w2)
+
+        z3 = keep.tile([P, 2, 2, NCH, 2], BF16, name="z3")
+        gw3 = new_grp()
+        banks3 = []
+
+        def run_w3():
+            for g in range(2):
+                for u in range(2):
+                    banks3.append(trs_pe(c3, g, u))
+
+        def prep_w3():
+            il(z3, gw3)
+            qz(gw3, wcod[3], wscl[3])
+
+        jobs3 = [[lambda k=k: trs_sc(banks3[k // 2], z3, k // 4, (k // 2) % 2, k % 2)] for k in range(8)]
+        group(1, 1, pe_run=run_w3, sjobs=jobs3[0:4], vjobs={0: lambda: qz(gw2, wcod[2], wscl[2])})
+        group(0, 2, sjobs=jobs3[4:8])
+        group(1, 2, vjobs={2: prep_w3}, a_first=(3,), splits=((0, 2), (2, 4)), rsplits=((0, 2), (2, 4)))
+        group(0, 3, a_first=(0, 1, 2, 3), splits=((0, 2), (2, 4)), rsplits=((0, 2), (2, 4)))
+        group(1, 3, vd=(2, 3), splits=((0, 2), (2, 3), (3, 4)), rsplits=((0, 2), (2, 4)), a_first=(0, 1, 2, 3))

@@ -103,15 +103,14 @@ def tile_ropeattnlayer_pa_kernel(tc, x, w_qk_bytes, w_qk_scale, out_0, out_1, ou
             nc.vector.scalar_tensor_tensor(out=gneg[:].rearrange("p s i j -> p (s i j)"), in0=ff, scalar=0.5,
                                            in1=ff, op0=ALU.is_gt, op1=ALU.subtract)
 
-        cosT = keep.tile([P, 4, HALF, 2], F32, name="cosT")
-        sinT = keep.tile([P, 4, HALF, 2], F32, name="sinT")
+        tab = keep.tile([P, 4, 2, HALF, 2], F32, name="tab")
 
         def sines():
-            nc.scalar.activation(out=cosT[:], in_=gneg[:, 1].unsqueeze(3).to_broadcast([P, 4, HALF, 2]),
+            nc.scalar.activation(out=tab[:, :, 0], in_=gneg[:, 1].unsqueeze(3).to_broadcast([P, 4, HALF, 2]),
                                  func=ACTF.Sin, scale=-2.0 * math.pi)
-            nc.scalar.activation(out=sinT[:, :, :, 1:2], in_=gneg[:, 0].unsqueeze(3), func=ACTF.Sin,
+            nc.scalar.activation(out=tab[:, :, 1, :, 0:1], in_=gneg[:, 0].unsqueeze(3), func=ACTF.Sin,
                                  scale=-2.0 * math.pi)
-            nc.scalar.activation(out=sinT[:, :, :, 0:1], in_=gneg[:, 0].unsqueeze(3), func=ACTF.Sin,
+            nc.scalar.activation(out=tab[:, :, 1, :, 1:2], in_=gneg[:, 0].unsqueeze(3), func=ACTF.Sin,
                                  scale=2.0 * math.pi)
 
         xcod, xscl, wcod, wscl = [], [], [], []
@@ -220,10 +219,10 @@ def tile_ropeattnlayer_pa_kernel(tc, x, w_qk_bytes, w_qk_scale, out_0, out_1, ou
                 nc.scalar.copy(out=pt[:, :, i - i0, :], in_=accs[i][:].rearrange("p (h d) -> p h d", h=4))
                 put(d_raw, raws, i)
 
-            def add(eng, i, t1, t2):
+            def add(eng, i, tt):
                 pt, i0, i1 = ropes[i]
-                eng.tensor_tensor(out=pt[:, :, i - i0, :], in0=t1[:].rearrange("p h j e -> p h (j e)"),
-                                  in1=t2[:].rearrange("p h j e -> p h (j e)"), op=ALU.add)
+                eng.tensor_tensor(out=pt[:, :, i - i0, :].rearrange("p h (j e) -> p h j e", e=2), in0=tt[:, 0],
+                                  in1=tt[:, 1, :, :, ::-1], op=ALU.add)
                 put(d_rope, ropes, i)
 
             accs = []
@@ -239,29 +238,27 @@ def tile_ropeattnlayer_pa_kernel(tc, x, w_qk_bytes, w_qk_scale, out_0, out_1, ou
                 pe_run()
             late = []
             for i in range(4):
-                t1 = tmp.tile([P, 4, HALF, 2], F32, name="t1")
-                t2 = tmp.tile([P, 4, HALF, 2], F32, name="t2")
-                a4 = accs[i][:].rearrange("p (h j e) -> p h j e", h=4, e=2)
+                tt = tmp.tile([P, 2, 4, HALF, 2], F32, name="tt")
                 if len(a_first) > 0 and i == a_first[0]:
                     for k in a_first:
                         copy_raw(k)
-                nc.vector.tensor_tensor(out=t1[:], in0=a4, in1=cosT[:, i].unsqueeze(1).to_broadcast([P, 4, HALF, 2]),
+                nc.vector.tensor_tensor(out=tt[:].rearrange("p s h j e -> p s h (j e)"),
+                                        in0=accs[i][:].rearrange("p (h d) -> p h d", h=4).unsqueeze(1).to_broadcast([P, 2, 4, DH]),
+                                        in1=tab[:, i].rearrange("p s j e -> p s (j e)").unsqueeze(2).to_broadcast([P, 2, 4, DH]),
                                         op=ALU.mult)
-                nc.vector.tensor_tensor(out=t2[:], in0=a4[:, :, :, ::-1],
-                                        in1=sinT[:, i].unsqueeze(1).to_broadcast([P, 4, HALF, 2]), op=ALU.mult)
                 if i not in a_first:
                     copy_raw(i)
                 if vjobs is not None and i in vjobs:
                     vjobs[i]()
                 if i in vd:
-                    late.append((i, t1, t2))
+                    late.append((i, tt))
                 else:
-                    add(nc.gpsimd, i, t1, t2)
+                    add(nc.gpsimd, i, tt)
                 if sjobs is not None:
                     for job in sjobs[i]:
                         job()
-            for (i, t1, t2) in late:
-                add(nc.vector, i, t1, t2)
+            for (i, tt) in late:
+                add(nc.vector, i, tt)
 
         gx0 = new_grp()
         gw0 = new_grp()

@@ -20,6 +20,7 @@ ACTF = mybir.ActivationFunctionType
 P = 128
 NCH = 512
 HALF = DH // 2
+PAIRS = ((0, 2), (2, 4))
 
 
 def tile_ropeattnlayer_pa_kernel(tc, x, w_qk_bytes, w_qk_scale, out_0, out_1, out_2, out_3):
@@ -30,7 +31,7 @@ def tile_ropeattnlayer_pa_kernel(tc, x, w_qk_bytes, w_qk_scale, out_0, out_1, ou
         wcp = ctx.enter_context(tc.tile_pool(name="wcp", bufs=4))
         gpl = ctx.enter_context(tc.tile_pool(name="gpl", bufs=3))
         stg = ctx.enter_context(tc.tile_pool(name="stg", bufs=3))
-        tmp = ctx.enter_context(tc.tile_pool(name="tmp", bufs=4))
+        tmp = ctx.enter_context(tc.tile_pool(name="tmp", bufs=3))
         tpp = ctx.enter_context(tc.psum_pool(name="tpp", bufs=4))
         mmp = ctx.enter_context(tc.psum_pool(name="mmp", bufs=4))
         ctx.enter_context(tc.manual_schedule())
@@ -192,7 +193,7 @@ def tile_ropeattnlayer_pa_kernel(tc, x, w_qk_bytes, w_qk_scale, out_0, out_1, ou
             jobs = [[lambda k=k: tr_cp(banks[k], grp, k % 2, k // 2)] for k in range(4)]
             return grp, pe_run, jobs
 
-        def group(b, c, pe_run=None, sjobs=None, vjobs=None, vd=(), splits=((0, 4),), rsplits=((0, 4),), a_first=()):
+        def group(b, c, pe_run=None, sjobs=None, vjobs=None, vd=(), cuts=PAIRS, splits=((0, 4),), rsplits=((0, 4),), a_first=()):
             d_raw = out_0 if c < 2 else out_1
             d_rope = out_2 if c < 2 else out_3
             h0 = 4 * (c % 2)
@@ -207,6 +208,9 @@ def tile_ropeattnlayer_pa_kernel(tc, x, w_qk_bytes, w_qk_scale, out_0, out_1, ou
 
             raws = pieces("raw", rsplits)
             ropes = pieces("rope", splits)
+            last_of = {}
+            for (a0, a1) in cuts:
+                last_of[a1 - 1] = a0
 
             def put(dst, where, i):
                 pt, i0, i1 = where[i]
@@ -219,11 +223,13 @@ def tile_ropeattnlayer_pa_kernel(tc, x, w_qk_bytes, w_qk_scale, out_0, out_1, ou
                 nc.scalar.copy(out=pt[:, :, i - i0, :], in_=accs[i][:].rearrange("p (h d) -> p h d", h=4))
                 put(d_raw, raws, i)
 
-            def add(eng, i, tt):
-                pt, i0, i1 = ropes[i]
-                eng.tensor_tensor(out=pt[:, :, i - i0, :].rearrange("p h (j e) -> p h j e", e=2), in0=tt[:, 0],
-                                  in1=tt[:, 1, :, :, ::-1], op=ALU.add)
-                put(d_rope, ropes, i)
+            def add(eng, a0, a1, tt):
+                pt, i0, i1 = ropes[a0]
+                k0 = a0 % 2
+                k1 = k0 + a1 - a0
+                eng.tensor_tensor(out=pt[:, :, a0 - i0:a1 - i0, :].rearrange("p h k (j e) -> p k h j e", e=2),
+                                  in0=tt[:, k0:k1, 0], in1=tt[:, k0:k1, 1, :, :, ::-1], op=ALU.add)
+                put(d_rope, ropes, a1 - 1)
 
             accs = []
             for i in range(4):
@@ -238,11 +244,12 @@ def tile_ropeattnlayer_pa_kernel(tc, x, w_qk_bytes, w_qk_scale, out_0, out_1, ou
                 pe_run()
             late = []
             for i in range(4):
-                tt = tmp.tile([P, 2, 4, HALF, 2], F32, name="tt")
+                if i % 2 == 0:
+                    tt = tmp.tile([P, 2, 2, 4, HALF, 2], F32, name="tt")
                 if len(a_first) > 0 and i == a_first[0]:
                     for k in a_first:
                         copy_raw(k)
-                nc.vector.tensor_tensor(out=tt[:].rearrange("p s h j e -> p s h (j e)"),
+                nc.vector.tensor_tensor(out=tt[:, i % 2].rearrange("p s h j e -> p s h (j e)"),
                                         in0=accs[i][:].rearrange("p (h d) -> p h d", h=4).unsqueeze(1).to_broadcast([P, 2, 4, DH]),
                                         in1=tab[:, i].rearrange("p s j e -> p s (j e)").unsqueeze(2).to_broadcast([P, 2, 4, DH]),
                                         op=ALU.mult)
@@ -250,15 +257,16 @@ def tile_ropeattnlayer_pa_kernel(tc, x, w_qk_bytes, w_qk_scale, out_0, out_1, ou
                     copy_raw(i)
                 if vjobs is not None and i in vjobs:
                     vjobs[i]()
-                if i in vd:
-                    late.append((i, tt))
-                else:
-                    add(nc.gpsimd, i, tt)
+                if i in last_of:
+                    if i in vd:
+                        late.append((last_of[i], i + 1, tt))
+                    else:
+                        add(nc.gpsimd, last_of[i], i + 1, tt)
                 if sjobs is not None:
                     for job in sjobs[i]:
                         job()
-            for (i, tt) in late:
-                add(nc.vector, i, tt)
+            for (a0, a1, tt) in late:
+                add(nc.vector, a0, a1, tt)
 
         gx0 = new_grp()
         gw0 = new_grp()
@@ -313,4 +321,4 @@ def tile_ropeattnlayer_pa_kernel(tc, x, w_qk_bytes, w_qk_scale, out_0, out_1, ou
         group(0, 2, sjobs=jobs3[4:8])
         group(1, 2, vjobs={2: prep_w3}, a_first=(3,), splits=((0, 2), (2, 4)), rsplits=((0, 2), (2, 4)))
         group(0, 3, a_first=(0, 1, 2, 3), splits=((0, 2), (2, 4)), rsplits=((0, 2), (2, 4)))
-        group(1, 3, vd=(2, 3), splits=((0, 2), (2, 3), (3, 4)), rsplits=((0, 2), (2, 4)), a_first=(0, 1, 2, 3))
+        group(1, 3, vd=(2, 3), cuts=((0, 2), (2, 3), (3, 4)), splits=((0, 2), (2, 3), (3, 4)), rsplits=((0, 2), (2, 4)), a_first=(0, 1, 2, 3))

from contextlib import ExitStack
import math

import concourse.mybir as mybir
from concourse.masks import make_identity

B, T, C, H, DH = 2, 512, 1024, 8, 128
FLOPS = 2 * B * T * C * 2 * C

F32 = mybir.dt.float32
BF16 = mybir.dt.bfloat16
U32 = mybir.dt.uint32
U8 = mybir.dt.uint8
I32 = mybir.dt.int32
FP8 = mybir.dt.float8_e4m3fn
FP8X4 = mybir.dt.float8_e4m3fn_x4
ALU = mybir.AluOpType
ACTF = mybir.ActivationFunctionType

P = 128
NCH = 512
HALF = DH // 2
PAIRS = ((0, 2), (2, 4))


def tile_ropeattnlayer_pa_kernel(tc, x, w_qk_bytes, w_qk_scale, out_0, out_1, out_2, out_3):
    nc = tc.nc
    with ExitStack() as ctx:
        keep = ctx.enter_context(tc.tile_pool(name="keep", bufs=1))
        wsp = ctx.enter_context(tc.tile_pool(name="wsp", bufs=8))
        wcp = ctx.enter_context(tc.tile_pool(name="wcp", bufs=4))
        gpl = ctx.enter_context(tc.tile_pool(name="gpl", bufs=3))
        stg = ctx.enter_context(tc.tile_pool(name="stg", bufs=3))
        tmp = ctx.enter_context(tc.tile_pool(name="tmp", bufs=3))
        tpp = ctx.enter_context(tc.psum_pool(name="tpp", bufs=4))
        mmp = ctx.enter_context(tc.psum_pool(name="mmp", bufs=4))
        ctx.enter_context(tc.manual_schedule())

        sc_bc = keep.tile([P, C], F32, name="sc_bc")
        nc.sync.dma_start(out=sc_bc[:], in_=w_qk_scale.rearrange("o k -> (o k)").partition_broadcast(P))
        sc4 = keep.tile([P, 2, 4], F32, name="sc4")
        wb = []
        for c in range(4):
            wbt = keep.tile([P, 4, C], U8, name="wb%d" % c)
            wb.append(wbt)
        xs = []
        for b in range(B):
            for hf in range(2):
                xst = keep.tile([P, 2, C], BF16, name="xs%d%d" % (b, hf))
                xs.append(xst)

        wb00 = keep.tile([P, C], U8, name="wb00")

        def load_w(c, r0=0, r1=4):
            wv = w_qk_bytes[NCH * c:NCH * (c + 1), :].rearrange("(r p) k -> p r k", p=P)
            nc.sync.dma_start(out=wb[c][:, r0:r1, :], in_=wv[:, r0:r1, :])

        def load_x(b):
            xv = x[b].rearrange("(p i) k -> p i k", i=4)
            for hf in range(2):
                nc.sync.dma_start(out=xs[2 * b + hf][:], in_=xv[:, 2 * hf:2 * hf + 2, :])

        nc.sync.dma_start(out=wb00[:], in_=w_qk_bytes[0:P, :])
        load_w(0, 1, 4)
        load_x(0)
        load_w(1)
        load_x(1)
        nc.sync.dma_start(out=sc4[:], in_=w_qk_scale.rearrange("o (g p t) -> p (o g) t", p=P, t=4))
        load_w(3)
        load_w(2)

        warm = keep.tile([P, 1], F32, name="warm")
        warm2 = keep.tile([P, 1], F32, name="warm2")
        nc.vector.memset(warm[:], 0.0)
        nc.scalar.activation(out=warm2[:], in_=warm[:], func=ACTF.Sin)

        q1 = 1000.0 ** (-2.0 / DH)
        pos = keep.tile([P, 4, 1], F32, name="pos")
        nc.gpsimd.iota(pos[:], pattern=[[1, 4]], base=1, channel_multiplier=4, allow_small_or_imprecise_dtypes=True)
        ident = keep.tile([P, P], F32, name="ident")
        make_identity(nc, ident[:])

        tau = keep.tile([P, 4, HALF], F32, name="tau")
        for j in range(4):
            nc.vector.tensor_scalar(out=tau[:, :, j:j + 1], in0=pos[:], scalar1=q1 ** (j + 1) / (2.0 * math.pi),
                                    scalar2=None, op0=ALU.mult)
        w = 4
        while w < HALF:
            nc.vector.tensor_scalar(out=tau[:, :, w:2 * w], in0=tau[:, :, 0:w], scalar1=q1 ** w, scalar2=None,
                                    op0=ALU.mult)
            w *= 2
        tau_f = tau[:].rearrange("p i j -> p (i j)")
        kint = keep.tile([P, 4 * HALF], I32, name="kint")
        kflt = keep.tile([P, 4 * HALF], F32, name="kflt")
        frac = keep.tile([P, 2, 4 * HALF], F32, name="frac")
        gneg = keep.tile([P, 2, 4, HALF], F32, name="gneg")
        nc.vector.tensor_copy(out=kint[:], in_=tau_f)
        nc.vector.tensor_copy(out=kflt[:], in_=kint[:])
        nc.vector.tensor_tensor(out=frac[:, 0, :], in0=tau_f, in1=kflt[:], op=ALU.subtract)
        nc.vector.tensor_scalar(out=frac[:, 1, :], in0=frac[:, 0, :], scalar1=0.25, scalar2=None, op0=ALU.add)

        def fold():
            ff = frac[:].rearrange("p s n -> p (s n)")
            nc.vector.scalar_tensor_tensor(out=gneg[:].rearrange("p s i j -> p (s i j)"), in0=ff, scalar=0.5,
                                           in1=ff, op0=ALU.is_gt, op1=ALU.subtract)

        tab = keep.tile([P, 4, 2, HALF, 2], F32, name="tab")

        def sines():
            nc.scalar.activation(out=tab[:, :, 0], in_=gneg[:, 1].unsqueeze(3).to_broadcast([P, 4, HALF, 2]),
                                 func=ACTF.Sin, scale=-2.0 * math.pi)
            nc.scalar.activation(out=tab[:, :, 1, :, 0:1], in_=gneg[:, 0].unsqueeze(3), func=ACTF.Sin,
                                 scale=-2.0 * math.pi)
            nc.scalar.activation(out=tab[:, :, 1, :, 1:2], in_=gneg[:, 0].unsqueeze(3), func=ACTF.Sin,
                                 scale=2.0 * math.pi)

        xcod, xscl, wcod, wscl = [], [], [], []
        for b in range(B):
            tcod = keep.tile([P, 2, NCH], U32, name="xcod%d" % b, align_bytes=64)
            tscl = keep.tile([P, 2, NCH], U8, name="xscl%d" % b, align_bytes=64)
            xcod.append(tcod)
            xscl.append(tscl)
        for c in range(4):
            tcod = keep.tile([P, 2, NCH], U32, name="wcod%d" % c, align_bytes=64)
            tscl = keep.tile([P, 2, NCH], U8, name="wscl%d" % c, align_bytes=64)
            wcod.append(tcod)
            wscl.append(tscl)

        def wtt(c, r):
            ws = wsp.tile([P, C], BF16, name="ws")
            src = wb00[:] if (c == 0 and r == 0) else wb[c][:, r, :]
            nc.vector.tensor_tensor(out=ws[:], in0=src.bitcast(FP8), in1=sc_bc[:], op=ALU.mult)
            return ws[:]

        def cast(c, r):
            wc = wcp.tile([P, C], BF16, name="wc")
            nc.scalar.copy(out=wc[:], in_=wb[c][:, r, :].bitcast(FP8))
            return wc[:]

        def new_grp():
            grp = gpl.tile([P, 2, NCH, 4], BF16, name="grp", align_bytes=64)
            return grp

        def tr_pe(srcs, g, hf):
            bank = tpp.tile([P, 2, 2, P], F32, name="bank")
            for a in range(2):
                words = srcs[2 * hf + a].bitcast(F32)
                for u in range(2):
                    nc.tensor.transpose(bank[:, a, u, :], words[:, 256 * g + u:256 * (g + 1):2], ident[:])
            return bank

        def tr_cp(bank, grp, g, hf):
            gw = grp[:, g].rearrange("p c t -> p (c t)").bitcast(F32)
            nc.scalar.copy(out=gw[:, 512 * hf:512 * (hf + 1)].rearrange("p (a q u) -> p a q u", a=2, u=2),
                           in_=bank[:].rearrange("p a u q -> p a q u"))

        def tr(srcs, grp, g, hf):
            tr_cp(tr_pe(srcs, g, hf), grp, g, hf)

        def trs_pe(srcs, g, u):
            bank = tpp.tile([P, 4, P], F32, name="bank")
            for r in range(4):
                nc.tensor.transpose(bank[:, r, :], srcs[r].bitcast(F32)[:, 256 * g + u:256 * (g + 1):2], ident[:])
            return bank

        def trs_sc(bank, z, g, u, e):
            src = bank[:].rearrange("p r q -> p (r q)").bitcast(BF16).rearrange("p (c e) -> p c e", e=2)
            nc.scalar.activation(out=z[:, g, u, :, e], in_=src[:, :, e], func=ACTF.Copy,
                                 scale=sc4[:, g, 2 * u + e:2 * u + e + 1])

        def il(z, grp):
            zin = z[:].rearrange("p g u c e -> p (g u c e)").bitcast(F32).rearrange("p (g u c) -> p g c u", g=2, u=2)
            gout = grp[:].rearrange("p g c t -> p (g c t)").bitcast(F32).rearrange("p (g c u) -> p g c u", g=2, u=2)
            nc.vector.tensor_copy(out=gout, in_=zin)

        def qz(grp, cod, scl):
            nc.vector.quantize_mx(out=cod[:].rearrange("p g c -> p (g c)").bitcast(FP8X4),
                                  scales=scl[:].rearrange("p g c -> p (g c)"),
                                  in_=grp[:].rearrange("p g c t -> p (g c t)"))

        def x_srcs(b):
            return [xs[2 * b + i // 2][:, i % 2, :] for i in range(4)]

        def plain_unit(srcs):
            grp = new_grp()
            banks = []

            def pe_run():
                for hf in range(2):
                    for g in range(2):
                        banks.append(tr_pe(srcs, g, hf))

            jobs = [[lambda k=k: tr_cp(banks[k], grp, k % 2, k // 2)] for k in range(4)]
            return grp, pe_run, jobs

        def group(b, c, pe_run=None, sjobs=None, vjobs=None, vd=(), cuts=PAIRS, splits=((0, 4),), rsplits=((0, 4),), a_first=()):
            d_raw = out_0 if c < 2 else out_1
            d_rope = out_2 if c < 2 else out_3
            h0 = 4 * (c % 2)

            def pieces(tag, cuts):
                where = {}
                for (i0, i1) in cuts:
                    pt = stg.tile([P, 4, i1 - i0, DH], F32, name=(tag if i1 - i0 == 4 else tag + "h"))
                    for i in range(i0, i1):
                        where[i] = (pt, i0, i1)
                return where

            raws = pieces("raw", rsplits)
            ropes = pieces("rope", splits)
            last_of = {}
            for (a0, a1) in cuts:
                last_of[a1 - 1] = a0

            def put(dst, where, i):
                pt, i0, i1 = where[i]
                if i == i1 - 1:
                    nc.sync.dma_start(out=dst[b, h0:h0 + 4].rearrange("h (p i) d -> p h i d", i=4)[:, :, i0:i1, :],
                                      in_=pt[:])

            def copy_raw(i):
                pt, i0, i1 = raws[i]
                nc.scalar.copy(out=pt[:, :, i - i0, :], in_=accs[i][:].rearrange("p (h d) -> p h d", h=4))
                put(d_raw, raws, i)

            def add(eng, a0, a1, tt):
                pt, i0, i1 = ropes[a0]
                k0 = a0 % 2
                k1 = k0 + a1 - a0
                eng.tensor_tensor(out=pt[:, :, a0 - i0:a1 - i0, :].rearrange("p h k (j e) -> p k h j e", e=2),
                                  in0=tt[:, k0:k1, 0], in1=tt[:, k0:k1, 1, :, :, ::-1], op=ALU.add)
                put(d_rope, ropes, a1 - 1)

            accs = []
            for i in range(4):
                acc = mmp.tile([P, NCH], F32, name="acc")
                accs.append(acc)
                for g in range(2):
                    nc.tensor.matmul_mx(out=acc[:], lhsT=xcod[b][:, g, i * P:(i + 1) * P].bitcast(FP8X4),
                                        lhsT_scale=xscl[b][:, g, i * P:(i + 1) * P],
                                        rhs=wcod[c][:, g, :].bitcast(FP8X4),
                                        rhs_scale=wscl[c][:, g, :], start=(g == 0), stop=(g == 1))
            if pe_run is not None:
                pe_run()
            late = []
            for i in range(4):
                if i % 2 == 0:
                    tt = tmp.tile([P, 2, 2, 4, HALF, 2], F32, name="tt")
                if len(a_first) > 0 and i == a_first[0]:
                    for k in a_first:
                        copy_raw(k)
                nc.vector.tensor_tensor(out=tt[:, i % 2].rearrange("p s h j e -> p s h (j e)"),
                                        in0=accs[i][:].rearrange("p (h d) -> p h d", h=4).unsqueeze(1).to_broadcast([P, 2, 4, DH]),
                                        in1=tab[:, i].rearrange("p s j e -> p s (j e)").unsqueeze(2).to_broadcast([P, 2, 4, DH]),
                                        op=ALU.mult)
                if i not in a_first:
                    copy_raw(i)
                if vjobs is not None and i in vjobs:
                    vjobs[i]()
                if i in last_of:
                    if i in vd:
                        late.append((last_of[i], i + 1, tt))
                    else:
                        add(nc.gpsimd, last_of[i], i + 1, tt)
                if sjobs is not None:
                    for job in sjobs[i]:
                        job()
            for (a0, a1, tt) in late:
                add(nc.vector, a0, a1, tt)

        gx0 = new_grp()
        gw0 = new_grp()
        gw1 = new_grp()
        s0 = [wtt(0, 0), wtt(0, 1)]
        fold()
        for hf in range(2):
            for g in range(2):
                tr(x_srcs(0), gx0, g, hf)
        tr(s0, gw0, 0, 0)
        tr(s0, gw0, 1, 0)
        sines()
        s0.append(wtt(0, 2))
        s0.append(wtt(0, 3))
        tr(s0, gw0, 0, 1)
        tr(s0, gw0, 1, 1)
        s1 = [wtt(1, 0), wtt(1, 1)]
        tr(s1, gw1, 0, 0)
        tr(s1, gw1, 1, 0)
        s1.append(wtt(1, 2))
        s1.append(wtt(1, 3))
        tr(s1, gw1, 0, 1)
        tr(s1, gw1, 1, 1)
        qz(gx0, xcod[0], xscl[0])
        qz(gw0, wcod[0], wscl[0])
        qz(gw1, wcod[1], wscl[1])

        gx1, run_x1, jobs_x1 = plain_unit(x_srcs(1))
        group(0, 0, pe_run=run_x1, sjobs=jobs_x1)
        c3 = []
        group(0, 1, vjobs={0: lambda: qz(gx1, xcod[1], xscl[1])},
              sjobs=[[lambda r=r: c3.append(cast(3, r))] for r in range(4)])
        s2 = [wtt(2, r) for r in range(4)]
        gw2, run_w2, jobs_w2 = plain_unit(s2)
        group(1, 0, pe_run=run_w2, sjobs=jobs_w2)

        z3 = keep.tile([P, 2, 2, NCH, 2], BF16, name="z3")
        gw3 = new_grp()
        banks3 = []

        def run_w3():
            for g in range(2):
                for u in range(2):
                    banks3.append(trs_pe(c3, g, u))

        def prep_w3():
            il(z3, gw3)
            qz(gw3, wcod[3], wscl[3])

        jobs3 = [[lambda k=k: trs_sc(banks3[k // 2], z3, k // 4, (k // 2) % 2, k % 2)] for k in range(8)]
        group(1, 1, pe_run=run_w3, sjobs=jobs3[0:4], vjobs={0: lambda: qz(gw2, wcod[2], wscl[2])})
        group(0, 2, sjobs=jobs3[4:8])
        group(1, 2, vjobs={2: prep_w3}, a_first=(3,), splits=((0, 2), (2, 4)), rsplits=((0, 2), (2, 4)))
        group(0, 3, a_first=(0, 1, 2, 3), splits=((0, 2), (2, 4)), rsplits=((0, 2), (2, 4)))
        group(1, 3, vd=(2, 3), cuts=((0, 2), (2, 3), (3, 4)), splits=((0, 2), (2, 3), (3, 4)), rsplits=((0, 2), (2, 4)), a_first=(0, 1, 2, 3))
